import numpy as np
import ml_dtypes


def mxq(x, axis, fmt="e4m3"):
    dtype, down = {"e4m3": (ml_dtypes.float8_e4m3fn, 7), "e5m2": (ml_dtypes.float8_e5m2, 14)}[fmt]
    v = np.moveaxis(np.asarray(x, np.float32).astype(ml_dtypes.bfloat16).astype(np.float64), axis, -1)
    blocks = v.reshape(v.shape[:-1] + (-1, 32))
    amax = np.abs(blocks).max(-1, keepdims=True)
    byte = np.maximum(np.where(amax > 0, np.frexp(amax)[1] - 1 + 127, 0) - down, 1)
    scale = np.exp2(byte - 127.0)
    codes = (blocks / scale).astype(np.float32).astype(dtype).astype(np.float64)
    return np.moveaxis((codes * scale).reshape(v.shape), -1, axis)


BF16 = ml_dtypes.bfloat16


def bf(x):
    return np.asarray(x, np.float32).astype(BF16)


def f64(x):
    return np.asarray(x).astype(np.float64)


N, D, K = 512, 512, 512
S = 5.0


def setup_inputs():
    m = np.random.standard_normal(D) / np.sqrt(D)
    return {"data": bf(m + np.random.standard_normal((N, D)) * 0.4 / np.sqrt(D)),
            "centers": bf(m + np.random.standard_normal((K, D)) * 0.4 / np.sqrt(D))}


def reference(data, centers):
    data, centers = f64(data), f64(centers)
    x2 = np.sum(data * data, axis=-1, keepdims=True)
    c2 = np.sum(centers * centers, axis=-1)[None, :]
    xc = mxq(data, 1, "e4m3") @ mxq(centers, 1, "e4m3").T
    r2 = x2 + c2 - 2.0 * xc
    rbfs = np.exp(-S * r2)
    ones = np.ones((data.shape[0], 1))
    return np.concatenate([ones, data, rbfs], axis=-1)

@@ -1,0 +1,137 @@
+from contextlib import ExitStack
+
+import concourse.mybir as mybir
+from concourse.masks import make_identity
+
+F32 = mybir.dt.float32
+BF16 = mybir.dt.bfloat16
+U32 = mybir.dt.uint32
+U8 = mybir.dt.uint8
+FP8X4 = mybir.dt.float8_e4m3fn_x4
+ACT = mybir.ActivationFunctionType
+ALU = mybir.AluOpType
+
+P = 128
+N, D, K = 512, 512, 512
+S = 5.0
+TILES = N // P
+PACK = 4
+WORDS = D // 2
+HALVES = WORDS // P
+PAIR = 2 * P
+PAD = 7
+
+FLOPS = 2 * N * D * K
+
+
+def tile_dicgaussianrbf_s_kernel(tc, data, centers, out):
+    nc = tc.nc
+    with ExitStack() as ctx:
+        keep = ctx.enter_context(tc.tile_pool(name="keep", bufs=1))
+        work = ctx.enter_context(tc.tile_pool(name="work", bufs=2))
+        psum_t = ctx.enter_context(tc.psum_pool(name="psum_t", bufs=3))
+        psum_c = ctx.enter_context(tc.psum_pool(name="psum_c", bufs=1))
+        psum_mx = ctx.enter_context(tc.psum_pool(name="psum_mx", bufs=TILES))
+
+        c_rows = [keep.tile([P, D], BF16, name="c_rows%d" % t) for t in range(TILES)]
+        d_rows = [keep.tile([P, D], BF16, name="d_rows%d" % t) for t in range(TILES)]
+        for t in range(TILES):
+            nc.sync.dma_start(out=c_rows[t][:], in_=centers[t * P : (t + 1) * P, :])
+        for t in range(TILES):
+            nc.sync.dma_start(out=d_rows[t][:], in_=data[t * P : (t + 1) * P, :])
+
+        ident = keep.tile([P, P], F32)
+        make_identity(nc, ident[:])
+        zero = keep.tile([P, 1], F32)
+        one = keep.tile([P, 1], F32)
+        nc.vector.memset(zero[:], 0.0)
+        nc.scalar.activation(out=one[:], in_=zero[:], func=ACT.Exp)
+        head = keep.tile([P, TILES, PAD + 1 + D], F32)
+        nc.vector.memset(head[:, :, PAD : PAD + 1], 1.0)
+
+        squares = keep.tile([P, 2 * TILES, D], BF16)
+        c2 = keep.tile([P, TILES], F32)
+        x2 = keep.tile([P, TILES], F32)
+
+        def row_norms(rows, t, scratch, sums):
+            nc.scalar.activation(out=scratch, in_=rows[t][:], func=ACT.Square, accum_out=sums[:, t : t + 1])
+
+        def features_to_partitions(rows, pair, grouped):
+            planes = psum_t.tile([P, HALVES, PAIR], F32, tag="planes")
+            for h in range(2):
+                words = rows[2 * pair + h][:].bitcast(F32)
+                for u in range(HALVES):
+                    nc.tensor.transpose(
+                        out=planes[:, u, h * P : (h + 1) * P],
+                        in_=words[:, u * P : (u + 1) * P],
+                        identity=ident[:],
+                    )
+            grouped_words = grouped[:].bitcast(F32)[:, pair * HALVES * PAIR : (pair + 1) * HALVES * PAIR]
+            nc.vector.tensor_copy(
+                out=grouped_words.rearrange("p (r u) -> p r u", u=HALVES),
+                in_=planes[:].rearrange("p u r -> p r u"),
+            )
+
+        def quantise(grouped, pair, codes, scales):
+            nc.vector.quantize_mx(
+                out=codes[:, pair * PAIR : (pair + 1) * PAIR].bitcast(FP8X4),
+                scales=scales[:, pair * PAIR : (pair + 1) * PAIR],
+                in_=grouped[:, pair * PAIR * PACK : (pair + 1) * PAIR * PACK],
+            )
+
+        c_grouped = keep.tile([P, K * PACK], BF16, align_bytes=64)
+        d_grouped = keep.tile([P, N * PACK], BF16, align_bytes=64)
+        c_codes = keep.tile([P, K], U32, align_bytes=64)
+        d_codes = keep.tile([P, N], U32, align_bytes=64)
+        c_scales = keep.tile([P, K], U8, align_bytes=64)
+        d_scales = keep.tile([P, N], U8, align_bytes=64)
+
+        for t in range(TILES):
+            row_norms(c_rows, t, squares[:, t, :], c2)
+        for pair in range(TILES // 2):
+            features_to_partitions(c_rows, pair, c_grouped)
+        for pair in range(TILES // 2):
+            quantise(c_grouped, pair, c_codes, c_scales)
+
+        for pair in range(TILES // 2):
+            features_to_partitions(d_rows, pair, d_grouped)
+        for pair in range(TILES // 2):
+            quantise(d_grouped, pair, d_codes, d_scales)
+        for t in range(TILES):
+            row_norms(d_rows, t, squares[:, TILES + t, :], x2)
+        for t in range(TILES):
+            nc.vector.tensor_copy(out=head[:, t, PAD + 1 :], in_=d_rows[t][:])
+            nc.sync.dma_start(out=out[t * P : (t + 1) * P, 0 : 1 + D], in_=head[:, t, PAD:])
+
+        c2_psum = psum_c.tile([P, K], F32)
+        for t in range(TILES):
+            nc.tensor.transpose(
+                out=c2_psum[:, t * P : (t + 1) * P],
+                in_=c2[:, t : t + 1].to_broadcast([P, P]),
+                identity=ident[:],
+            )
+        c2_all = keep.tile([P, K], F32)
+        nc.scalar.copy(out=c2_all[:], in_=c2_psum[:])
+        bias = keep.tile([P, TILES], F32)
+        nc.vector.tensor_scalar_mul(out=bias[:], in0=x2[:], scalar1=-S)
+
+        rbf = keep.tile([P, TILES, K], F32)
+        for t in range(TILES):
+            xc = psum_mx.tile([P, K], F32, tag="xc")
+            nc.tensor.matmul_mx(
+                out=xc[:],
+                lhsT=d_codes[:, t * P : (t + 1) * P].bitcast(FP8X4),
+                lhsT_scale=d_scales[:, t * P : (t + 1) * P],
+                rhs=c_codes[:].bitcast(FP8X4),
+                rhs_scale=c_scales[:],
+                start=True,
+                stop=True,
+            )
+            c2_minus_2xc = work.tile([P, K], F32, tag="c2_minus_2xc")
+            nc.vector.scalar_tensor_tensor(
+                out=c2_minus_2xc[:], in0=xc[:], scalar=-2.0, in1=c2_all[:], op0=ALU.mult, op1=ALU.add
+            )
+            nc.scalar.activation(
+                out=rbf[:, t, :], in_=c2_minus_2xc[:], func=ACT.Exp, scale=-S, bias=bias[:, t : t + 1]
+            )
+            nc.sync.dma_start(out=out[t * P : (t + 1) * P, 1 + D :], in_=rbf[:, t, :])

@@ -35,28 +35,30 @@ def tile_dicgaussianrbf_s_kernel(tc, data, centers, out):
 
         c_rows = [keep.tile([P, D], BF16, name="c_rows%d" % t) for t in range(TILES)]
         d_rows = [keep.tile([P, D], BF16, name="d_rows%d" % t) for t in range(TILES)]
-        for t in range(TILES):
-            nc.sync.dma_start(out=c_rows[t][:], in_=centers[t * P : (t + 1) * P, :])
-        for t in range(TILES):
-            nc.sync.dma_start(out=d_rows[t][:], in_=data[t * P : (t + 1) * P, :])
-
         ident = keep.tile([P, P], F32)
-        make_identity(nc, ident[:])
         zero = keep.tile([P, 1], F32)
         one = keep.tile([P, 1], F32)
-        nc.vector.memset(zero[:], 0.0)
-        nc.scalar.activation(out=one[:], in_=zero[:], func=ACT.Exp)
         head = keep.tile([P, TILES, PAD + 1 + D], F32)
-        nc.vector.memset(head[:, :, PAD : PAD + 1], 1.0)
-
         squares = keep.tile([P, 2 * TILES, D], BF16)
         c2 = keep.tile([P, TILES], F32)
         x2 = keep.tile([P, TILES], F32)
+        bias = keep.tile([P, TILES], F32)
+        c2_all = keep.tile([P, K], F32)
+        c_grouped = keep.tile([P, K * PACK], BF16, align_bytes=64)
+        d_grouped = keep.tile([P, N * PACK], BF16, align_bytes=64)
+        c_codes = keep.tile([P, K], U32, align_bytes=64)
+        d_codes = keep.tile([P, N], U32, align_bytes=64)
+        c_scales = keep.tile([P, K], U8, align_bytes=64)
+        d_scales = keep.tile([P, N], U8, align_bytes=64)
+        rbf = keep.tile([P, TILES, K], F32)
 
-        def row_norms(rows, t, scratch, sums):
+        def rows_of(t):
+            return slice(t * P, (t + 1) * P)
+
+        def row_norm(rows, t, scratch, sums):
             nc.scalar.activation(out=scratch, in_=rows[t][:], func=ACT.Square, accum_out=sums[:, t : t + 1])
 
-        def features_to_partitions(rows, pair, grouped):
+        def transposes(rows, pair):
             planes = psum_t.tile([P, HALVES, PAIR], F32, tag="planes")
             for h in range(2):
                 words = rows[2 * pair + h][:].bitcast(F32)
@@ -66,6 +68,9 @@ def tile_dicgaussianrbf_s_kernel(tc, data, centers, out):
                         in_=words[:, u * P : (u + 1) * P],
                         identity=ident[:],
                     )
+            return planes
+
+        def group(planes, pair, grouped):
             grouped_words = grouped[:].bitcast(F32)[:, pair * HALVES * PAIR : (pair + 1) * HALVES * PAIR]
             nc.vector.tensor_copy(
                 out=grouped_words.rearrange("p (r u) -> p r u", u=HALVES),
@@ -79,59 +84,73 @@ def tile_dicgaussianrbf_s_kernel(tc, data, centers, out):
                 in_=grouped[:, pair * PAIR * PACK : (pair + 1) * PAIR * PACK],
             )
 
-        c_grouped = keep.tile([P, K * PACK], BF16, align_bytes=64)
-        d_grouped = keep.tile([P, N * PACK], BF16, align_bytes=64)
-        c_codes = keep.tile([P, K], U32, align_bytes=64)
-        d_codes = keep.tile([P, N], U32, align_bytes=64)
-        c_scales = keep.tile([P, K], U8, align_bytes=64)
-        d_scales = keep.tile([P, N], U8, align_bytes=64)
-
-        for t in range(TILES):
-            row_norms(c_rows, t, squares[:, t, :], c2)
-        for pair in range(TILES // 2):
-            features_to_partitions(c_rows, pair, c_grouped)
-        for pair in range(TILES // 2):
-            quantise(c_grouped, pair, c_codes, c_scales)
-
-        for pair in range(TILES // 2):
-            features_to_partitions(d_rows, pair, d_grouped)
-        for pair in range(TILES // 2):
-            quantise(d_grouped, pair, d_codes, d_scales)
-        for t in range(TILES):
-            row_norms(d_rows, t, squares[:, TILES + t, :], x2)
-        for t in range(TILES):
+        def widen(t):
             nc.vector.tensor_copy(out=head[:, t, PAD + 1 :], in_=d_rows[t][:])
-            nc.sync.dma_start(out=out[t * P : (t + 1) * P, 0 : 1 + D], in_=head[:, t, PAD:])
+            nc.sync.dma_start(out=out[rows_of(t), 0 : 1 + D], in_=head[:, t, PAD:])
 
-        c2_psum = psum_c.tile([P, K], F32)
-        for t in range(TILES):
-            nc.tensor.transpose(
-                out=c2_psum[:, t * P : (t + 1) * P],
-                in_=c2[:, t : t + 1].to_broadcast([P, P]),
-                identity=ident[:],
-            )
-        c2_all = keep.tile([P, K], F32)
-        nc.scalar.copy(out=c2_all[:], in_=c2_psum[:])
-        bias = keep.tile([P, TILES], F32)
-        nc.vector.tensor_scalar_mul(out=bias[:], in0=x2[:], scalar1=-S)
-
-        rbf = keep.tile([P, TILES, K], F32)
-        for t in range(TILES):
+        def finish(t):
             xc = psum_mx.tile([P, K], F32, tag="xc")
             nc.tensor.matmul_mx(
                 out=xc[:],
-                lhsT=d_codes[:, t * P : (t + 1) * P].bitcast(FP8X4),
-                lhsT_scale=d_scales[:, t * P : (t + 1) * P],
+                lhsT=d_codes[:, rows_of(t)].bitcast(FP8X4),
+                lhsT_scale=d_scales[:, rows_of(t)],
                 rhs=c_codes[:].bitcast(FP8X4),
                 rhs_scale=c_scales[:],
                 start=True,
                 stop=True,
             )
             c2_minus_2xc = work.tile([P, K], F32, tag="c2_minus_2xc")
+            nc.vector.tensor_scalar_mul(out=bias[:, t : t + 1], in0=x2[:, t : t + 1], scalar1=-S)
             nc.vector.scalar_tensor_tensor(
                 out=c2_minus_2xc[:], in0=xc[:], scalar=-2.0, in1=c2_all[:], op0=ALU.mult, op1=ALU.add
             )
             nc.scalar.activation(
                 out=rbf[:, t, :], in_=c2_minus_2xc[:], func=ACT.Exp, scale=-S, bias=bias[:, t : t + 1]
             )
-            nc.sync.dma_start(out=out[t * P : (t + 1) * P, 1 + D :], in_=rbf[:, t, :])
+            nc.sync.dma_start(out=out[rows_of(t), 1 + D :], in_=rbf[:, t, :])
+
+        ctx.enter_context(tc.manual_schedule())
+
+        for t in range(TILES):
+            nc.sync.dma_start(out=c_rows[t][:], in_=centers[rows_of(t), :])
+        for t in range(TILES):
+            nc.sync.dma_start(out=d_rows[t][:], in_=data[rows_of(t), :])
+
+        make_identity(nc, ident[:])
+        nc.vector.memset(zero[:], 0.0)
+        nc.scalar.activation(out=one[:], in_=zero[:], func=ACT.Exp)
+        nc.vector.memset(head[:, :, PAD : PAD + 1], 1.0)
+
+        for t in range(TILES):
+            row_norm(c_rows, t, squares[:, t, :], c2)
+        row_norm(d_rows, 0, squares[:, TILES, :], x2)
+
+        c_planes = [transposes(c_rows, pair) for pair in range(2)]
+        group(c_planes[0], 0, c_grouped)
+        group(c_planes[1], 1, c_grouped)
+        d_planes0 = transposes(d_rows, 0)
+        quantise(c_grouped, 0, c_codes, c_scales)
+        group(d_planes0, 0, d_grouped)
+        quantise(c_grouped, 1, c_codes, c_scales)
+        d_planes1 = transposes(d_rows, 1)
+        group(d_planes1, 1, d_grouped)
+        quantise(d_grouped, 0, d_codes, d_scales)
+        widen(0)
+        quantise(d_grouped, 1, d_codes, d_scales)
+        widen(1)
+
+        c2_psum = psum_c.tile([P, K], F32)
+        for t in range(TILES):
+            nc.tensor.transpose(
+                out=c2_psum[:, rows_of(t)], in_=c2[:, t : t + 1].to_broadcast([P, P]), identity=ident[:]
+            )
+        nc.scalar.copy(out=c2_all[:], in_=c2_psum[:])
+        for t in range(1, TILES):
+            row_norm(d_rows, t, squares[:, TILES + t, :], x2)
+
+        finish(0)
+        widen(2)
+        finish(1)
+        widen(3)
+        finish(2)
+        finish(3)

@@ -1,3 +1,4 @@
+import math
 from contextlib import ExitStack
 
 import concourse.mybir as mybir
@@ -28,7 +29,7 @@ def tile_dicgaussianrbf_s_kernel(tc, data, centers, out):
     nc = tc.nc
     with ExitStack() as ctx:
         keep = ctx.enter_context(tc.tile_pool(name="keep", bufs=1))
-        work = ctx.enter_context(tc.tile_pool(name="work", bufs=2))
+        work = ctx.enter_context(tc.tile_pool(name="work", bufs=TILES))
         psum_t = ctx.enter_context(tc.psum_pool(name="psum_t", bufs=3))
         psum_c = ctx.enter_context(tc.psum_pool(name="psum_c", bufs=1))
         psum_mx = ctx.enter_context(tc.psum_pool(name="psum_mx", bufs=TILES))
@@ -39,11 +40,11 @@ def tile_dicgaussianrbf_s_kernel(tc, data, centers, out):
         zero = keep.tile([P, 1], F32)
         one = keep.tile([P, 1], F32)
         head = keep.tile([P, TILES, PAD + 1 + D], F32)
+        unit = keep.tile([P, 1], F32)
         squares = keep.tile([P, 2 * TILES, D], BF16)
-        c2 = keep.tile([P, TILES], F32)
-        x2 = keep.tile([P, TILES], F32)
-        bias = keep.tile([P, TILES], F32)
-        c2_all = keep.tile([P, K], F32)
+        half_c2 = keep.tile([P, TILES], F32)
+        half_x2 = keep.tile([P, TILES], F32)
+        half_c2_all = keep.tile([P, K], F32)
         c_grouped = keep.tile([P, K * PACK], BF16, align_bytes=64)
         d_grouped = keep.tile([P, N * PACK], BF16, align_bytes=64)
         c_codes = keep.tile([P, K], U32, align_bytes=64)
@@ -56,7 +57,20 @@ def tile_dicgaussianrbf_s_kernel(tc, data, centers, out):
             return slice(t * P, (t + 1) * P)
 
         def row_norm(rows, t, scratch, sums):
-            nc.scalar.activation(out=scratch, in_=rows[t][:], func=ACT.Square, accum_out=sums[:, t : t + 1])
+            nc.scalar.activation(
+                out=scratch, in_=rows[t][:], func=ACT.Square, scale=math.sqrt(0.5), accum_out=sums[:, t : t + 1]
+            )
+
+        def row_norm_on_vector(rows, t, scratch, sums):
+            nc.vector.scalar_tensor_tensor(
+                out=scratch,
+                in0=rows[t][:],
+                scalar=0.5,
+                in1=rows[t][:],
+                op0=ALU.mult,
+                op1=ALU.mult,
+                accum_out=sums[:, t : t + 1],
+            )
 
         def transposes(rows, pair):
             planes = psum_t.tile([P, HALVES, PAIR], F32, tag="planes")
@@ -70,9 +84,9 @@ def tile_dicgaussianrbf_s_kernel(tc, data, centers, out):
                     )
             return planes
 
-        def group(planes, pair, grouped):
+        def group(engine_copy, planes, pair, grouped):
             grouped_words = grouped[:].bitcast(F32)[:, pair * HALVES * PAIR : (pair + 1) * HALVES * PAIR]
-            nc.vector.tensor_copy(
+            engine_copy(
                 out=grouped_words.rearrange("p (r u) -> p r u", u=HALVES),
                 in_=planes[:].rearrange("p u r -> p r u"),
             )
@@ -84,8 +98,10 @@ def tile_dicgaussianrbf_s_kernel(tc, data, centers, out):
                 in_=grouped[:, pair * PAIR * PACK : (pair + 1) * PAIR * PACK],
             )
 
-        def widen(t):
-            nc.vector.tensor_copy(out=head[:, t, PAD + 1 :], in_=d_rows[t][:])
+        def widen(t, unit):
+            nc.gpsimd.tensor_scalar(
+                out=head[:, t, PAD + 1 :], in0=d_rows[t][:], scalar1=unit, scalar2=unit, op0=ALU.mult, op1=ALU.mult
+            )
             nc.sync.dma_start(out=out[rows_of(t), 0 : 1 + D], in_=head[:, t, PAD:])
 
         def finish(t):
@@ -99,14 +115,16 @@ def tile_dicgaussianrbf_s_kernel(tc, data, centers, out):
                 start=True,
                 stop=True,
             )
-            c2_minus_2xc = work.tile([P, K], F32, tag="c2_minus_2xc")
-            nc.vector.tensor_scalar_mul(out=bias[:, t : t + 1], in0=x2[:, t : t + 1], scalar1=-S)
+            minus_half_r2 = work.tile([P, K], F32, tag="minus_half_r2")
             nc.vector.scalar_tensor_tensor(
-                out=c2_minus_2xc[:], in0=xc[:], scalar=-2.0, in1=c2_all[:], op0=ALU.mult, op1=ALU.add
+                out=minus_half_r2[:],
+                in0=xc[:],
+                scalar=half_x2[:, t : t + 1],
+                in1=half_c2_all[:],
+                op0=ALU.subtract,
+                op1=ALU.subtract,
             )
-            nc.scalar.activation(
-                out=rbf[:, t, :], in_=c2_minus_2xc[:], func=ACT.Exp, scale=-S, bias=bias[:, t : t + 1]
-            )
+            nc.scalar.activation(out=rbf[:, t, :], in_=minus_half_r2[:], func=ACT.Exp, scale=2.0 * S)
             nc.sync.dma_start(out=out[rows_of(t), 1 + D :], in_=rbf[:, t, :])
 
         ctx.enter_context(tc.manual_schedule())
@@ -121,36 +139,37 @@ def tile_dicgaussianrbf_s_kernel(tc, data, centers, out):
         nc.scalar.activation(out=one[:], in_=zero[:], func=ACT.Exp)
         nc.vector.memset(head[:, :, PAD : PAD + 1], 1.0)
 
-        for t in range(TILES):
-            row_norm(c_rows, t, squares[:, t, :], c2)
-        row_norm(d_rows, 0, squares[:, TILES, :], x2)
+        row_norm_on_vector(c_rows, 1, squares[:, 1, :], half_c2)
+        for t in (0, 2, 3):
+            row_norm(c_rows, t, squares[:, t, :], half_c2)
+        row_norm(d_rows, 0, squares[:, TILES, :], half_x2)
+
+        for t in (0, 1):
+            widen(t, 1.0)
 
         c_planes = [transposes(c_rows, pair) for pair in range(2)]
-        group(c_planes[0], 0, c_grouped)
-        group(c_planes[1], 1, c_grouped)
+        group(nc.vector.tensor_copy, c_planes[0], 0, c_grouped)
+        group(nc.vector.tensor_copy, c_planes[1], 1, c_grouped)
         d_planes0 = transposes(d_rows, 0)
+        group(nc.scalar.copy, d_planes0, 0, d_grouped)
         quantise(c_grouped, 0, c_codes, c_scales)
-        group(d_planes0, 0, d_grouped)
         quantise(c_grouped, 1, c_codes, c_scales)
-        d_planes1 = transposes(d_rows, 1)
-        group(d_planes1, 1, d_grouped)
         quantise(d_grouped, 0, d_codes, d_scales)
-        widen(0)
-        quantise(d_grouped, 1, d_codes, d_scales)
-        widen(1)
-
-        c2_psum = psum_c.tile([P, K], F32)
+        nc.vector.memset(unit[:], 1.0)
+        half_c2_psum = psum_c.tile([P, K], F32)
         for t in range(TILES):
             nc.tensor.transpose(
-                out=c2_psum[:, rows_of(t)], in_=c2[:, t : t + 1].to_broadcast([P, P]), identity=ident[:]
+                out=half_c2_psum[:, rows_of(t)], in_=half_c2[:, t : t + 1].to_broadcast([P, P]), identity=ident[:]
             )
-        nc.scalar.copy(out=c2_all[:], in_=c2_psum[:])
+        nc.scalar.copy(out=half_c2_all[:], in_=half_c2_psum[:])
+        d_planes1 = transposes(d_rows, 1)
+        group(nc.vector.tensor_copy, d_planes1, 1, d_grouped)
         for t in range(1, TILES):
-            row_norm(d_rows, t, squares[:, TILES + t, :], x2)
-
+            row_norm(d_rows, t, squares[:, TILES + t, :], half_x2)
+        for t in (2, 3):
+            widen(t, unit[:])
         finish(0)
-        widen(2)
-        finish(1)
-        widen(3)
-        finish(2)
-        finish(3)
+        quantise(d_grouped, 1, d_codes, d_scales)
+
+        for t in range(1, TILES):
+            finish(t)

@@ -40,7 +40,6 @@ def tile_dicgaussianrbf_s_kernel(tc, data, centers, out):
         zero = keep.tile([P, 1], F32)
         one = keep.tile([P, 1], F32)
         head = keep.tile([P, TILES, PAD + 1 + D], F32)
-        unit = keep.tile([P, 1], F32)
         squares = keep.tile([P, 2 * TILES, D], BF16)
         half_c2 = keep.tile([P, TILES], F32)
         half_x2 = keep.tile([P, TILES], F32)
@@ -91,17 +90,15 @@ def tile_dicgaussianrbf_s_kernel(tc, data, centers, out):
                 in_=planes[:].rearrange("p u r -> p r u"),
             )
 
-        def quantise(grouped, pair, codes, scales):
+        def quantise(grouped, first, end, codes, scales):
+            rows = slice(first * PAIR, end * PAIR)
             nc.vector.quantize_mx(
-                out=codes[:, pair * PAIR : (pair + 1) * PAIR].bitcast(FP8X4),
-                scales=scales[:, pair * PAIR : (pair + 1) * PAIR],
-                in_=grouped[:, pair * PAIR * PACK : (pair + 1) * PAIR * PACK],
+                out=codes[:, rows].bitcast(FP8X4),
+                scales=scales[:, rows],
+                in_=grouped[:, first * PAIR * PACK : end * PAIR * PACK],
             )
 
-        def widen(t, unit):
-            nc.gpsimd.tensor_scalar(
-                out=head[:, t, PAD + 1 :], in0=d_rows[t][:], scalar1=unit, scalar2=unit, op0=ALU.mult, op1=ALU.mult
-            )
+        def store_head(t):
             nc.sync.dma_start(out=out[rows_of(t), 0 : 1 + D], in_=head[:, t, PAD:])
 
         def finish(t):
@@ -142,34 +139,35 @@ def tile_dicgaussianrbf_s_kernel(tc, data, centers, out):
         row_norm_on_vector(c_rows, 1, squares[:, 1, :], half_c2)
         for t in (0, 2, 3):
             row_norm(c_rows, t, squares[:, t, :], half_c2)
-        row_norm(d_rows, 0, squares[:, TILES, :], half_x2)
-
         for t in (0, 1):
-            widen(t, 1.0)
+            row_norm(d_rows, t, squares[:, TILES + t, :], half_x2)
 
         c_planes = [transposes(c_rows, pair) for pair in range(2)]
         group(nc.vector.tensor_copy, c_planes[0], 0, c_grouped)
         group(nc.vector.tensor_copy, c_planes[1], 1, c_grouped)
         d_planes0 = transposes(d_rows, 0)
-        group(nc.scalar.copy, d_planes0, 0, d_grouped)
-        quantise(c_grouped, 0, c_codes, c_scales)
-        quantise(c_grouped, 1, c_codes, c_scales)
-        quantise(d_grouped, 0, d_codes, d_scales)
-        nc.vector.memset(unit[:], 1.0)
+        group(nc.vector.tensor_copy, d_planes0, 0, d_grouped)
+        for t in (0, 1, 2):
+            nc.gpsimd.tensor_scalar(
+                out=head[:, t, PAD + 1 :], in0=d_rows[t][:], scalar1=1.0, scalar2=1.0, op0=ALU.mult, op1=ALU.mult
+            )
+            store_head(t)
+        d_planes1 = transposes(d_rows, 1)
+        group(nc.scalar.copy, d_planes1, 1, d_grouped)
+        quantise(c_grouped, 0, 2, c_codes, c_scales)
+        quantise(d_grouped, 0, 1, d_codes, d_scales)
+        quantise(d_grouped, 1, 2, d_codes, d_scales)
+        nc.vector.tensor_copy(out=head[:, 3, PAD + 1 :], in_=d_rows[3][:])
+        store_head(3)
+
         half_c2_psum = psum_c.tile([P, K], F32)
         for t in range(TILES):
             nc.tensor.transpose(
                 out=half_c2_psum[:, rows_of(t)], in_=half_c2[:, t : t + 1].to_broadcast([P, P]), identity=ident[:]
             )
         nc.scalar.copy(out=half_c2_all[:], in_=half_c2_psum[:])
-        d_planes1 = transposes(d_rows, 1)
-        group(nc.vector.tensor_copy, d_planes1, 1, d_grouped)
-        for t in range(1, TILES):
-            row_norm(d_rows, t, squares[:, TILES + t, :], half_x2)
         for t in (2, 3):
-            widen(t, unit[:])
-        finish(0)
-        quantise(d_grouped, 1, d_codes, d_scales)
+            row_norm(d_rows, t, squares[:, TILES + t, :], half_x2)
 
-        for t in range(1, TILES):
+        for t in range(TILES):
             finish(t)

@@ -40,6 +40,7 @@ def tile_dicgaussianrbf_s_kernel(tc, data, centers, out):
         zero = keep.tile([P, 1], F32)
         one = keep.tile([P, 1], F32)
         head = keep.tile([P, TILES, PAD + 1 + D], F32)
+        unit = keep.tile([P, 16], F32)
         squares = keep.tile([P, 2 * TILES, D], BF16)
         half_c2 = keep.tile([P, TILES], F32)
         half_x2 = keep.tile([P, TILES], F32)
@@ -90,15 +91,17 @@ def tile_dicgaussianrbf_s_kernel(tc, data, centers, out):
                 in_=planes[:].rearrange("p u r -> p r u"),
             )
 
-        def quantise(grouped, first, end, codes, scales):
-            rows = slice(first * PAIR, end * PAIR)
+        def quantise(grouped, pair, codes, scales):
             nc.vector.quantize_mx(
-                out=codes[:, rows].bitcast(FP8X4),
-                scales=scales[:, rows],
-                in_=grouped[:, first * PAIR * PACK : end * PAIR * PACK],
+                out=codes[:, pair * PAIR : (pair + 1) * PAIR].bitcast(FP8X4),
+                scales=scales[:, pair * PAIR : (pair + 1) * PAIR],
+                in_=grouped[:, pair * PAIR * PACK : (pair + 1) * PAIR * PACK],
             )
 
-        def store_head(t):
+        def widen(t, unit):
+            nc.gpsimd.tensor_scalar(
+                out=head[:, t, PAD + 1 :], in0=d_rows[t][:], scalar1=unit, scalar2=unit, op0=ALU.mult, op1=ALU.mult
+            )
             nc.sync.dma_start(out=out[rows_of(t), 0 : 1 + D], in_=head[:, t, PAD:])
 
         def finish(t):
@@ -136,38 +139,36 @@ def tile_dicgaussianrbf_s_kernel(tc, data, centers, out):
         nc.scalar.activation(out=one[:], in_=zero[:], func=ACT.Exp)
         nc.vector.memset(head[:, :, PAD : PAD + 1], 1.0)
 
-        row_norm_on_vector(c_rows, 1, squares[:, 1, :], half_c2)
-        for t in (0, 2, 3):
+        for t in (0, 2):
+            row_norm_on_vector(c_rows, t, squares[:, t, :], half_c2)
+        for t in (1, 3):
             row_norm(c_rows, t, squares[:, t, :], half_c2)
-        for t in (0, 1):
-            row_norm(d_rows, t, squares[:, TILES + t, :], half_x2)
+        row_norm(d_rows, 0, squares[:, TILES, :], half_x2)
 
         c_planes = [transposes(c_rows, pair) for pair in range(2)]
-        group(nc.vector.tensor_copy, c_planes[0], 0, c_grouped)
-        group(nc.vector.tensor_copy, c_planes[1], 1, c_grouped)
-        d_planes0 = transposes(d_rows, 0)
-        group(nc.vector.tensor_copy, d_planes0, 0, d_grouped)
-        for t in (0, 1, 2):
-            nc.gpsimd.tensor_scalar(
-                out=head[:, t, PAD + 1 :], in0=d_rows[t][:], scalar1=1.0, scalar2=1.0, op0=ALU.mult, op1=ALU.mult
-            )
-            store_head(t)
-        d_planes1 = transposes(d_rows, 1)
-        group(nc.scalar.copy, d_planes1, 1, d_grouped)
-        quantise(c_grouped, 0, 2, c_codes, c_scales)
-        quantise(d_grouped, 0, 1, d_codes, d_scales)
-        quantise(d_grouped, 1, 2, d_codes, d_scales)
-        nc.vector.tensor_copy(out=head[:, 3, PAD + 1 :], in_=d_rows[3][:])
-        store_head(3)
-
+        d_planes = [transposes(d_rows, pair) for pair in range(2)]
+        for pair in range(2):
+            group(nc.vector.tensor_copy, c_planes[pair], pair, c_grouped)
+        for pair in range(2):
+            group(nc.scalar.copy, d_planes[pair], pair, d_grouped)
+        for t in range(1, TILES):
+            row_norm(d_rows, t, squares[:, TILES + t, :], half_x2)
+        for t in (0, 1):
+            widen(t, 1.0)
+        quantise(c_grouped, 0, c_codes, c_scales)
+        quantise(c_grouped, 1, c_codes, c_scales)
+        quantise(d_grouped, 0, d_codes, d_scales)
         half_c2_psum = psum_c.tile([P, K], F32)
         for t in range(TILES):
             nc.tensor.transpose(
                 out=half_c2_psum[:, rows_of(t)], in_=half_c2[:, t : t + 1].to_broadcast([P, P]), identity=ident[:]
             )
-        nc.scalar.copy(out=half_c2_all[:], in_=half_c2_psum[:])
-        for t in (2, 3):
-            row_norm(d_rows, t, squares[:, TILES + t, :], half_x2)
+        nc.vector.memset(unit[:, 0:1], 1.0)
+        widen(2, unit[:, 0:1])
+        nc.vector.tensor_copy(out=half_c2_all[:], in_=half_c2_psum[:])
+        quantise(d_grouped, 1, d_codes, d_scales)
+        nc.vector.memset(unit[:, 8:9], 1.0)
+        widen(3, unit[:, 8:9])
 
         for t in range(TILES):
             finish(t)

@@ -30,9 +30,9 @@ def tile_dicgaussianrbf_s_kernel(tc, data, centers, out):
     with ExitStack() as ctx:
         keep = ctx.enter_context(tc.tile_pool(name="keep", bufs=1))
         work = ctx.enter_context(tc.tile_pool(name="work", bufs=TILES))
-        psum_t = ctx.enter_context(tc.psum_pool(name="psum_t", bufs=3))
+        psum_t = ctx.enter_context(tc.psum_pool(name="psum_t", bufs=4))
         psum_c = ctx.enter_context(tc.psum_pool(name="psum_c", bufs=1))
-        psum_mx = ctx.enter_context(tc.psum_pool(name="psum_mx", bufs=TILES))
+        psum_mx = ctx.enter_context(tc.psum_pool(name="psum_mx", bufs=3))
 
         c_rows = [keep.tile([P, D], BF16, name="c_rows%d" % t) for t in range(TILES)]
         d_rows = [keep.tile([P, D], BF16, name="d_rows%d" % t) for t in range(TILES)]
@@ -72,30 +72,31 @@ def tile_dicgaussianrbf_s_kernel(tc, data, centers, out):
                 accum_out=sums[:, t : t + 1],
             )
 
-        def transposes(rows, pair):
-            planes = psum_t.tile([P, HALVES, PAIR], F32, tag="planes")
-            for h in range(2):
-                words = rows[2 * pair + h][:].bitcast(F32)
+        def transposes(rows, first, end):
+            planes = psum_t.tile([P, HALVES, (end - first) * P], F32, tag="planes")
+            for t in range(first, end):
+                words = rows[t][:].bitcast(F32)
                 for u in range(HALVES):
                     nc.tensor.transpose(
-                        out=planes[:, u, h * P : (h + 1) * P],
+                        out=planes[:, u, (t - first) * P : (t - first + 1) * P],
                         in_=words[:, u * P : (u + 1) * P],
                         identity=ident[:],
                     )
             return planes
 
-        def group(engine_copy, planes, pair, grouped):
-            grouped_words = grouped[:].bitcast(F32)[:, pair * HALVES * PAIR : (pair + 1) * HALVES * PAIR]
+        def group(engine_copy, planes, first, end, grouped):
+            grouped_words = grouped[:].bitcast(F32)[:, first * HALVES * P : end * HALVES * P]
             engine_copy(
                 out=grouped_words.rearrange("p (r u) -> p r u", u=HALVES),
                 in_=planes[:].rearrange("p u r -> p r u"),
             )
 
-        def quantise(grouped, pair, codes, scales):
+        def quantise(grouped, first, end, codes, scales):
+            rows = slice(first * P, end * P)
             nc.vector.quantize_mx(
-                out=codes[:, pair * PAIR : (pair + 1) * PAIR].bitcast(FP8X4),
-                scales=scales[:, pair * PAIR : (pair + 1) * PAIR],
-                in_=grouped[:, pair * PAIR * PACK : (pair + 1) * PAIR * PACK],
+                out=codes[:, rows].bitcast(FP8X4),
+                scales=scales[:, rows],
+                in_=grouped[:, first * P * PACK : end * P * PACK],
             )
 
         def widen(t, unit):
@@ -139,36 +140,36 @@ def tile_dicgaussianrbf_s_kernel(tc, data, centers, out):
         nc.scalar.activation(out=one[:], in_=zero[:], func=ACT.Exp)
         nc.vector.memset(head[:, :, PAD : PAD + 1], 1.0)
 
-        for t in (0, 2):
-            row_norm_on_vector(c_rows, t, squares[:, t, :], half_c2)
-        for t in (1, 3):
+        row_norm_on_vector(c_rows, 1, squares[:, 1, :], half_c2)
+        for t in (0, 2, 3):
             row_norm(c_rows, t, squares[:, t, :], half_c2)
         row_norm(d_rows, 0, squares[:, TILES, :], half_x2)
 
-        c_planes = [transposes(c_rows, pair) for pair in range(2)]
-        d_planes = [transposes(d_rows, pair) for pair in range(2)]
-        for pair in range(2):
-            group(nc.vector.tensor_copy, c_planes[pair], pair, c_grouped)
-        for pair in range(2):
-            group(nc.scalar.copy, d_planes[pair], pair, d_grouped)
+        for t in (0, 2):
+            group(nc.vector.tensor_copy, transposes(c_rows, t, t + 2), t, t + 2, c_grouped)
+        d_planes0 = transposes(d_rows, 0, 1)
+        d_planes1 = transposes(d_rows, 1, 2)
+        group(nc.vector.tensor_copy, d_planes1, 1, 2, d_grouped)
+        group(nc.scalar.copy, d_planes0, 0, 1, d_grouped)
+        group(nc.scalar.copy, transposes(d_rows, 2, 4), 2, 4, d_grouped)
         for t in range(1, TILES):
             row_norm(d_rows, t, squares[:, TILES + t, :], half_x2)
+
         for t in (0, 1):
             widen(t, 1.0)
-        quantise(c_grouped, 0, c_codes, c_scales)
-        quantise(c_grouped, 1, c_codes, c_scales)
-        quantise(d_grouped, 0, d_codes, d_scales)
+        quantise(c_grouped, 0, 4, c_codes, c_scales)
+        nc.vector.memset(unit[:, 0:1], 1.0)
+        widen(2, unit[:, 0:1])
+        quantise(d_grouped, 0, 2, d_codes, d_scales)
         half_c2_psum = psum_c.tile([P, K], F32)
         for t in range(TILES):
             nc.tensor.transpose(
                 out=half_c2_psum[:, rows_of(t)], in_=half_c2[:, t : t + 1].to_broadcast([P, P]), identity=ident[:]
             )
-        nc.vector.memset(unit[:, 0:1], 1.0)
-        widen(2, unit[:, 0:1])
         nc.vector.tensor_copy(out=half_c2_all[:], in_=half_c2_psum[:])
-        quantise(d_grouped, 1, d_codes, d_scales)
         nc.vector.memset(unit[:, 8:9], 1.0)
         widen(3, unit[:, 8:9])
+        quantise(d_grouped, 2, 4, d_codes, d_scales)
 
         for t in range(TILES):
             finish(t)

@@ -34,8 +34,10 @@ def tile_dicgaussianrbf_s_kernel(tc, data, centers, out):
         psum_c = ctx.enter_context(tc.psum_pool(name="psum_c", bufs=1))
         psum_mx = ctx.enter_context(tc.psum_pool(name="psum_mx", bufs=3))
 
-        c_rows = [keep.tile([P, D], BF16, name="c_rows%d" % t) for t in range(TILES)]
-        d_rows = [keep.tile([P, D], BF16, name="d_rows%d" % t) for t in range(TILES)]
+        c_all = keep.tile([P, TILES, D], BF16)
+        c_rows = [c_all[:, t, :] for t in range(TILES)]
+        d_all = keep.tile([P, TILES, D], BF16)
+        d_rows = [d_all[:, t, :] for t in range(TILES)]
         ident = keep.tile([P, P], F32)
         zero = keep.tile([P, 1], F32)
         one = keep.tile([P, 1], F32)
@@ -58,15 +60,15 @@ def tile_dicgaussianrbf_s_kernel(tc, data, centers, out):
 
         def row_norm(rows, t, scratch, sums):
             nc.scalar.activation(
-                out=scratch, in_=rows[t][:], func=ACT.Square, scale=math.sqrt(0.5), accum_out=sums[:, t : t + 1]
+                out=scratch, in_=rows[t], func=ACT.Square, scale=math.sqrt(0.5), accum_out=sums[:, t : t + 1]
             )
 
         def row_norm_on_vector(rows, t, scratch, sums):
             nc.vector.scalar_tensor_tensor(
                 out=scratch,
-                in0=rows[t][:],
+                in0=rows[t],
                 scalar=0.5,
-                in1=rows[t][:],
+                in1=rows[t],
                 op0=ALU.mult,
                 op1=ALU.mult,
                 accum_out=sums[:, t : t + 1],
@@ -75,7 +77,7 @@ def tile_dicgaussianrbf_s_kernel(tc, data, centers, out):
         def transposes(rows, first, end):
             planes = psum_t.tile([P, HALVES, (end - first) * P], F32, tag="planes")
             for t in range(first, end):
-                words = rows[t][:].bitcast(F32)
+                words = rows[t].bitcast(F32)
                 for u in range(HALVES):
                     nc.tensor.transpose(
                         out=planes[:, u, (t - first) * P : (t - first + 1) * P],
@@ -101,11 +103,11 @@ def tile_dicgaussianrbf_s_kernel(tc, data, centers, out):
 
         def widen(t, unit):
             nc.gpsimd.tensor_scalar(
-                out=head[:, t, PAD + 1 :], in0=d_rows[t][:], scalar1=unit, scalar2=unit, op0=ALU.mult, op1=ALU.mult
+                out=head[:, t, PAD + 1 :], in0=d_rows[t], scalar1=unit, scalar2=unit, op0=ALU.mult, op1=ALU.mult
             )
             nc.sync.dma_start(out=out[rows_of(t), 0 : 1 + D], in_=head[:, t, PAD:])
 
-        def finish(t):
+        def finish(t, pieces=1):
             xc = psum_mx.tile([P, K], F32, tag="xc")
             nc.tensor.matmul_mx(
                 out=xc[:],
@@ -117,23 +119,31 @@ def tile_dicgaussianrbf_s_kernel(tc, data, centers, out):
                 stop=True,
             )
             minus_half_r2 = work.tile([P, K], F32, tag="minus_half_r2")
-            nc.vector.scalar_tensor_tensor(
-                out=minus_half_r2[:],
-                in0=xc[:],
-                scalar=half_x2[:, t : t + 1],
-                in1=half_c2_all[:],
-                op0=ALU.subtract,
-                op1=ALU.subtract,
-            )
-            nc.scalar.activation(out=rbf[:, t, :], in_=minus_half_r2[:], func=ACT.Exp, scale=2.0 * S)
-            nc.sync.dma_start(out=out[rows_of(t), 1 + D :], in_=rbf[:, t, :])
+            width = K // pieces
+            for i in range(pieces):
+                cols = slice(i * width, (i + 1) * width)
+                nc.vector.scalar_tensor_tensor(
+                    out=minus_half_r2[:, cols],
+                    in0=xc[:, cols],
+                    scalar=half_x2[:, t : t + 1],
+                    in1=half_c2_all[:, cols],
+                    op0=ALU.subtract,
+                    op1=ALU.subtract,
+                )
+                nc.scalar.activation(
+                    out=rbf[:, t, cols], in_=minus_half_r2[:, cols], func=ACT.Exp, scale=2.0 * S
+                )
+                nc.sync.dma_start(
+                    out=out[rows_of(t), 1 + D + i * width : 1 + D + (i + 1) * width], in_=rbf[:, t, cols]
+                )
 
         ctx.enter_context(tc.manual_schedule())
 
         for t in range(TILES):
-            nc.sync.dma_start(out=c_rows[t][:], in_=centers[rows_of(t), :])
-        for t in range(TILES):
-            nc.sync.dma_start(out=d_rows[t][:], in_=data[rows_of(t), :])
+            nc.sync.dma_start(out=c_rows[t], in_=centers[rows_of(t), :])
+        for t in range(2):
+            nc.sync.dma_start(out=d_rows[t], in_=data[rows_of(t), :])
+        nc.sync.dma_start(out=d_all[:, 2:4, :], in_=data[2 * P : 4 * P, :].rearrange("(t p) d -> p t d", p=P))
 
         make_identity(nc, ident[:])
         nc.vector.memset(zero[:], 0.0)
@@ -171,5 +181,6 @@ def tile_dicgaussianrbf_s_kernel(tc, data, centers, out):
         widen(3, unit[:, 8:9])
         quantise(d_grouped, 2, 4, d_codes, d_scales)
 
-        for t in range(TILES):
+        finish(0, pieces=2)
+        for t in range(1, TILES):
             finish(t)

import math
from contextlib import ExitStack

import concourse.mybir as mybir
from concourse.masks import make_identity

F32 = mybir.dt.float32
BF16 = mybir.dt.bfloat16
U32 = mybir.dt.uint32
U8 = mybir.dt.uint8
FP8X4 = mybir.dt.float8_e4m3fn_x4
ACT = mybir.ActivationFunctionType
ALU = mybir.AluOpType

P = 128
N, D, K = 512, 512, 512
S = 5.0
TILES = N // P
PACK = 4
WORDS = D // 2
HALVES = WORDS // P
PAIR = 2 * P
PAD = 7

FLOPS = 2 * N * D * K


def tile_dicgaussianrbf_s_kernel(tc, data, centers, out):
    nc = tc.nc
    with ExitStack() as ctx:
        keep = ctx.enter_context(tc.tile_pool(name="keep", bufs=1))
        work = ctx.enter_context(tc.tile_pool(name="work", bufs=TILES))
        psum_t = ctx.enter_context(tc.psum_pool(name="psum_t", bufs=4))
        psum_c = ctx.enter_context(tc.psum_pool(name="psum_c", bufs=1))
        psum_mx = ctx.enter_context(tc.psum_pool(name="psum_mx", bufs=3))

        c_all = keep.tile([P, TILES, D], BF16)
        c_rows = [c_all[:, t, :] for t in range(TILES)]
        d_all = keep.tile([P, TILES, D], BF16)
        d_rows = [d_all[:, t, :] for t in range(TILES)]
        ident = keep.tile([P, P], F32)
        zero = keep.tile([P, 1], F32)
        one = keep.tile([P, 1], F32)
        head = keep.tile([P, TILES, PAD + 1 + D], F32)
        unit = keep.tile([P, 16], F32)
        squares = keep.tile([P, 2 * TILES, D], BF16)
        half_c2 = keep.tile([P, TILES], F32)
        half_x2 = keep.tile([P, TILES], F32)
        half_c2_all = keep.tile([P, K], F32)
        c_grouped = keep.tile([P, K * PACK], BF16, align_bytes=64)
        d_grouped = keep.tile([P, N * PACK], BF16, align_bytes=64)
        c_codes = keep.tile([P, K], U32, align_bytes=64)
        d_codes = keep.tile([P, N], U32, align_bytes=64)
        c_scales = keep.tile([P, K], U8, align_bytes=64)
        d_scales = keep.tile([P, N], U8, align_bytes=64)
        rbf = keep.tile([P, TILES, K], F32)

        def rows_of(t):
            return slice(t * P, (t + 1) * P)

        def row_norm(rows, t, scratch, sums):
            nc.scalar.activation(
                out=scratch, in_=rows[t], func=ACT.Square, scale=math.sqrt(0.5), accum_out=sums[:, t : t + 1]
            )

        def row_norm_on_vector(rows, t, scratch, sums):
            nc.vector.scalar_tensor_tensor(
                out=scratch,
                in0=rows[t],
                scalar=0.5,
                in1=rows[t],
                op0=ALU.mult,
                op1=ALU.mult,
                accum_out=sums[:, t : t + 1],
            )

        def transposes(rows, first, end):
            planes = psum_t.tile([P, HALVES, (end - first) * P], F32, tag="planes")
            for t in range(first, end):
                words = rows[t].bitcast(F32)
                for u in range(HALVES):
                    nc.tensor.transpose(
                        out=planes[:, u, (t - first) * P : (t - first + 1) * P],
                        in_=words[:, u * P : (u + 1) * P],
                        identity=ident[:],
                    )
            return planes

        def group(engine_copy, planes, first, end, grouped):
            grouped_words = grouped[:].bitcast(F32)[:, first * HALVES * P : end * HALVES * P]
            engine_copy(
                out=grouped_words.rearrange("p (r u) -> p r u", u=HALVES),
                in_=planes[:].rearrange("p u r -> p r u"),
            )

        def quantise(grouped, first, end, codes, scales):
            rows = slice(first * P, end * P)
            nc.vector.quantize_mx(
                out=codes[:, rows].bitcast(FP8X4),
                scales=scales[:, rows],
                in_=grouped[:, first * P * PACK : end * P * PACK],
            )

        def widen(t, unit):
            nc.gpsimd.tensor_scalar(
                out=head[:, t, PAD + 1 :], in0=d_rows[t], scalar1=unit, scalar2=unit, op0=ALU.mult, op1=ALU.mult
            )
            nc.sync.dma_start(out=out[rows_of(t), 0 : 1 + D], in_=head[:, t, PAD:])

        def finish(t, pieces=1):
            xc = psum_mx.tile([P, K], F32, tag="xc")
            nc.tensor.matmul_mx(
                out=xc[:],
                lhsT=d_codes[:, rows_of(t)].bitcast(FP8X4),
                lhsT_scale=d_scales[:, rows_of(t)],
                rhs=c_codes[:].bitcast(FP8X4),
                rhs_scale=c_scales[:],
                start=True,
                stop=True,
            )
            minus_half_r2 = work.tile([P, K], F32, tag="minus_half_r2")
            width = K // pieces
            for i in range(pieces):
                cols = slice(i * width, (i + 1) * width)
                nc.vector.scalar_tensor_tensor(
                    out=minus_half_r2[:, cols],
                    in0=xc[:, cols],
                    scalar=half_x2[:, t : t + 1],
                    in1=half_c2_all[:, cols],
                    op0=ALU.subtract,
                    op1=ALU.subtract,
                )
                nc.scalar.activation(
                    out=rbf[:, t, cols], in_=minus_half_r2[:, cols], func=ACT.Exp, scale=2.0 * S
                )
                nc.sync.dma_start(
                    out=out[rows_of(t), 1 + D + i * width : 1 + D + (i + 1) * width], in_=rbf[:, t, cols]
                )

        ctx.enter_context(tc.manual_schedule())

        for t in range(TILES):
            nc.sync.dma_start(out=c_rows[t], in_=centers[rows_of(t), :])
        for t in range(2):
            nc.sync.dma_start(out=d_rows[t], in_=data[rows_of(t), :])
        nc.sync.dma_start(out=d_all[:, 2:4, :], in_=data[2 * P : 4 * P, :].rearrange("(t p) d -> p t d", p=P))

        make_identity(nc, ident[:])
        nc.vector.memset(zero[:], 0.0)
        nc.scalar.activation(out=one[:], in_=zero[:], func=ACT.Exp)
        nc.vector.memset(head[:, :, PAD : PAD + 1], 1.0)

        row_norm_on_vector(c_rows, 1, squares[:, 1, :], half_c2)
        for t in (0, 2, 3):
            row_norm(c_rows, t, squares[:, t, :], half_c2)
        row_norm(d_rows, 0, squares[:, TILES, :], half_x2)

        for t in (0, 2):
            group(nc.vector.tensor_copy, transposes(c_rows, t, t + 2), t, t + 2, c_grouped)
        d_planes0 = transposes(d_rows, 0, 1)
        d_planes1 = transposes(d_rows, 1, 2)
        group(nc.vector.tensor_copy, d_planes1, 1, 2, d_grouped)
        group(nc.scalar.copy, d_planes0, 0, 1, d_grouped)
        group(nc.scalar.copy, transposes(d_rows, 2, 4), 2, 4, d_grouped)
        for t in range(1, TILES):
            row_norm(d_rows, t, squares[:, TILES + t, :], half_x2)

        for t in (0, 1):
            widen(t, 1.0)
        quantise(c_grouped, 0, 4, c_codes, c_scales)
        nc.vector.memset(unit[:, 0:1], 1.0)
        widen(2, unit[:, 0:1])
        quantise(d_grouped, 0, 2, d_codes, d_scales)
        half_c2_psum = psum_c.tile([P, K], F32)
        for t in range(TILES):
            nc.tensor.transpose(
                out=half_c2_psum[:, rows_of(t)], in_=half_c2[:, t : t + 1].to_broadcast([P, P]), identity=ident[:]
            )
        nc.vector.tensor_copy(out=half_c2_all[:], in_=half_c2_psum[:])
        nc.vector.memset(unit[:, 8:9], 1.0)
        widen(3, unit[:, 8:9])
        quantise(d_grouped, 2, 4, d_codes, d_scales)

        finish(0, pieces=2)
        for t in range(1, TILES):
            finish(t)
